import numpy as np
import ml_dtypes


def mxq(x, axis, fmt="e4m3"):
    dtype, down = {"e4m3": (ml_dtypes.float8_e4m3fn, 7), "e5m2": (ml_dtypes.float8_e5m2, 14)}[fmt]
    v = np.moveaxis(np.asarray(x, np.float32).astype(ml_dtypes.bfloat16).astype(np.float64), axis, -1)
    blocks = v.reshape(v.shape[:-1] + (-1, 32))
    amax = np.abs(blocks).max(-1, keepdims=True)
    byte = np.maximum(np.where(amax > 0, np.frexp(amax)[1] - 1 + 127, 0) - down, 1)
    scale = np.exp2(byte - 127.0)
    codes = (blocks / scale).astype(np.float32).astype(dtype).astype(np.float64)
    return np.moveaxis((codes * scale).reshape(v.shape), -1, axis)


WIDE = False


def mx_kscale(k):
    if not WIDE:
        return np.ones(k)
    levels = np.array([30, -30])
    if k % 512:
        return np.exp2(np.random.permutation(np.resize(levels, k // 32))).repeat(32)
    a = np.empty((k // 512, 16))
    for p in range(k // 512):
        a[p, :8] = np.random.permutation(np.resize(levels, 8))
        for g in range(8):
            far = levels[np.abs(levels - a[p, g]) >= 10]
            a[p, g + 8] = far[np.random.randint(len(far))]
    return np.exp2(a.ravel()).repeat(32)


BF16 = ml_dtypes.bfloat16


def bf(x):
    return np.asarray(x, np.float32).astype(BF16)


def f64(x):
    return np.asarray(x).astype(np.float64)


B, C, TC, H, W = 4, 512, 512, 32, 16
N = H * W
EPS = 1e-6


def setup_inputs():
    s = mx_kscale(TC)
    return {"token": bf(np.random.standard_normal((B, TC, H, W)) * s[None, :, None, None]),
            "Wk": bf(np.random.standard_normal((C, TC)) / np.sqrt(TC) / s[None, :]),
            "Wv": bf(np.random.standard_normal((C, TC)) * 3.0 / np.sqrt(TC) / s[None, :])}


def reference(token, Wk, Wv):
    tq = mxq(f64(token).reshape(B, TC, N), 1, "e5m2")
    kf = mxq(f64(Wk), 1, "e5m2") @ tq
    v = mxq(f64(Wv), 1, "e5m2") @ tq
    vf = v.transpose(0, 2, 1)
    kn = kf / np.maximum(np.sqrt((kf * kf).sum(1, keepdims=True)), EPS)
    return kn, vf

@@ -1,0 +1,278 @@
+from contextlib import ExitStack
+
+import concourse.mybir as mybir
+from concourse.masks import make_identity
+
+B, C, K, N = 4, 512, 512, 512
+EPS = 1e-6
+FLOPS = 2 * 2 * B * C * K * N
+
+F32 = mybir.dt.float32
+BF16 = mybir.dt.bfloat16
+U32 = mybir.dt.uint32
+U8 = mybir.dt.uint8
+E5M2X4 = mybir.dt.float8_e5m2_x4
+ACT = mybir.ActivationFunctionType
+ALU = mybir.AluOpType
+ENG = mybir.EngineType
+TINY = 2.0**-80
+
+P = 128
+PACK = 4
+TILES = 4
+HALF = 256
+
+
+def tile_trgramkqv_pa_kernel(tc, token, Wk, Wv, out_0, out_1):
+    nc = tc.nc
+    with ExitStack() as ctx:
+        keep = ctx.enter_context(tc.tile_pool(name="keep", bufs=1))
+        scratch = ctx.enter_context(tc.tile_pool(name="scratch", bufs=2))
+        psum = ctx.enter_context(tc.psum_pool(name="psum", bufs=1))
+        ctx.enter_context(tc.manual_schedule(engines={ENG.Activation, ENG.DVE, ENG.SP, ENG.Pool}))
+
+        def kept(name, shape, dtype):
+            return keep.tile(shape, dtype, name=name, align_bytes=64)
+
+        ident = kept("ident", [P, P], F32)
+        wv_raw = [kept("wv_raw%d" % a, [P, 2, K], BF16) for a in range(2)]
+        wk_raw = [kept("wk_raw%d" % h, [P, 2, K], BF16) for h in range(2)]
+        tiny = kept("tiny", [P, 1], F32)
+        one = kept("one", [P, 1], F32)
+        cap = kept("cap", [P, 1], F32)
+        tok_raw = [kept("tok_raw%d" % b, [P, PACK, N], BF16) for b in range(B)]
+        wv_grp = kept("wv_grp", [P, C * PACK], BF16)
+        wk_grp = kept("wk_grp", [P, C * PACK], BF16)
+        tok_grp = [kept("tok_grp%d" % b, [P, N * PACK], BF16) for b in range(B)]
+        wv_codes = kept("wv_codes", [P, C], U32)
+        wv_scales = kept("wv_scales", [P, C], U8)
+        wk_codes = kept("wk_codes", [P, C], U32)
+        wk_scales = kept("wk_scales", [P, C], U8)
+        tok_codes = [kept("tok_codes%d" % b, [P, N], U32) for b in range(B)]
+        tok_scales = [kept("tok_scales%d" % b, [P, N], U8) for b in range(B)]
+        v_sb = [kept("v_sb%d" % b, [P, TILES, C], F32) for b in range(B)]
+        k_sb = [kept("k_sb%d" % b, [P, TILES, N], F32) for b in range(B)]
+        sumsq = [kept("sumsq%d" % b, [P, TILES], F32) for b in range(B)]
+        inv_norm = [kept("inv_norm%d" % b, [P, N], F32) for b in range(B)]
+
+        def scalar_bank():
+            return psum.tile([P, 512], F32, name="scalar_bank", tag="scalar_bank", bufs=4)
+
+        def vector_bank():
+            return psum.tile([P, 512], F32, name="vector_bank", tag="vector_bank", bufs=3)
+
+        def load_token(b):
+            nc.sync.dma_start(out=tok_raw[b][:], in_=token[b].rearrange("(p j) h w -> p j (h w)", j=PACK))
+
+        def turn_weights(raw_pair, grp_half, order):
+            bank = scalar_bank()
+            turned = bank[:].rearrange("p (t u m) -> p t u m", t=2, u=2)
+            for t in range(2):
+                words = raw_pair[:, t, :].bitcast(F32)
+                for u in range(2):
+                    nc.tensor.transpose(turned[:, t, u, :], words[:, u : 2 * P : 2], ident[:])
+            nc.scalar.copy(
+                out=grp_half.bitcast(F32).rearrange("p (%s) -> p %s" % (order, order), t=2, u=2),
+                in_=turned.rearrange("p t u m -> p %s" % order),
+            )
+
+        def half_cols(a, scale=1):
+            return slice(a * HALF * scale, (a + 1) * HALF * scale)
+
+        def quantize(codes, scales, grp, a):
+            nc.vector.quantize_mx(
+                out=codes[:, half_cols(a)].bitcast(E5M2X4),
+                scales=scales[:, half_cols(a)],
+                in_=grp[:, half_cols(a, PACK)],
+            )
+
+        def quantize_whole(codes, scales, grp):
+            nc.vector.quantize_mx(out=codes[:].bitcast(E5M2X4), scales=scales[:], in_=grp[:])
+
+        def interleave(b, a):
+            grouped = tok_grp[b][:].rearrange("p (i a c m t) -> p a c t m i", i=2, a=2, m=2, t=PACK)
+            nc.vector.tensor_copy(
+                out=grouped[:, a],
+                in_=tok_raw[b][:, :, half_cols(a)].rearrange("p t (c m i) -> p c t m i", m=2, i=2),
+            )
+
+        def pixel_block(j):
+            return 2 * (j % 2) + j // 2
+
+        def quantize_token(b, a):
+            for i in range(2):
+                first = pixel_block(2 * a + i) * P
+                nc.vector.quantize_mx(
+                    out=tok_codes[b][:, first : first + P].bitcast(E5M2X4),
+                    scales=tok_scales[b][:, first : first + P],
+                    in_=tok_grp[b][:, first * PACK : (first + P) * PACK],
+                )
+
+        def product(bank, lhs_codes, lhs_scales, j, rhs_codes, rhs_scales):
+            cols = slice(j * P, (j + 1) * P)
+            nc.tensor.matmul_mx(
+                out=bank[:],
+                lhsT=lhs_codes[:, cols].bitcast(E5M2X4),
+                lhsT_scale=lhs_scales[:, cols],
+                rhs=rhs_codes[:].bitcast(E5M2X4),
+                rhs_scale=rhs_scales[:],
+                start=True,
+                stop=True,
+            )
+
+        def store_v(b, a):
+            nc.sync.dma_start(
+                out=out_1[b].rearrange("(a m i) c -> m a i c", a=2, i=2)[:, a, :, :],
+                in_=v_sb[b][:, 2 * a : 2 * a + 2, :],
+            )
+
+        def store_k(b, t, count):
+            nc.sync.dma_start(
+                out=out_0[b].rearrange("(m t) n -> m t n", t=TILES)[:, t : t + count, :],
+                in_=k_sb[b][:, t : t + count, :],
+            )
+
+        def v_on_scalar(b, j):
+            bank = scalar_bank()
+            product(bank, tok_codes[b], tok_scales[b], pixel_block(j), wv_codes, wv_scales)
+            nc.scalar.copy(out=v_sb[b][:, j, :], in_=bank[:])
+            if j % 2 == 1:
+                store_v(b, j // 2)
+
+        def v_on_vector(b, j):
+            bank = vector_bank()
+            product(bank, tok_codes[b], tok_scales[b], pixel_block(j), wv_codes, wv_scales)
+            nc.vector.tensor_copy(out=v_sb[b][:, j, :], in_=bank[:])
+            if j % 2 == 1:
+                store_v(b, j // 2)
+
+        def squares(b, j):
+            bank = scalar_bank()
+            product(bank, tok_codes[b], tok_scales[b], pixel_block(j), wk_codes, wk_scales)
+            squared = scratch.tile([P, C], F32, name="squared")
+            nc.scalar.activation(out=squared[:], in_=bank[:], func=ACT.Square, accum_out=sumsq[b][:, j : j + 1])
+
+        norm_banks = {}
+
+        def spread_sumsq(b):
+            bank = psum.tile([P, 512], F32, name="norm_bank", tag="norm_bank", bufs=1)
+            for j in range(TILES):
+                first = pixel_block(j) * P
+                nc.tensor.transpose(bank[:, first : first + P], sumsq[b][:, j : j + 1].to_broadcast([P, P]), ident[:])
+            norm_banks[b] = bank
+
+        def invert_norm(b):
+            nc.scalar.activation(
+                out=inv_norm[b][:].rearrange("p (m i) -> p m i", i=2),
+                in_=norm_banks[b][:].rearrange("p (i m) -> p m i", i=2),
+                func=ACT.Abs_reciprocal_sqrt,
+                bias=tiny[:],
+            )
+
+        def k_tile(b, t):
+            bank = vector_bank()
+            product(bank, wk_codes, wk_scales, t, tok_codes[b], tok_scales[b])
+            nc.vector.scalar_tensor_tensor(
+                out=k_sb[b][:, t, :].rearrange("p (m i) -> p m i", i=2),
+                in0=inv_norm[b][:].rearrange("p (m i) -> p m i", i=2),
+                scalar=cap[:],
+                in1=bank[:].rearrange("p (i m) -> p m i", i=2),
+                op0=ALU.min,
+                op1=ALU.mult,
+            )
+            if b == B - 1 and t >= 2:
+                store_k(b, t, 1)
+            elif t % 2 == 1:
+                store_k(b, t - 1, 2)
+
+        wv_rows = Wv.rearrange("(a m t) k -> m a t k", a=2, t=2)
+        for a in range(2):
+            nc.sync.dma_start(out=wv_raw[a][:], in_=wv_rows[:, a, :, :])
+        load_token(0)
+        wk_rows = Wk.rearrange("(m t) k -> m t k", t=PACK)
+        for h in range(2):
+            nc.sync.dma_start(out=wk_raw[h][:], in_=wk_rows[:, 2 * h : 2 * h + 2, :])
+        for b in range(1, B):
+            load_token(b)
+        nc.gpsimd.memset(one[:], 1.0)
+        nc.gpsimd.memset(tiny[:], TINY)
+        make_identity(nc, ident[:])
+        nc.scalar.activation(out=cap[:], in_=one[:], func=ACT.Abs_reciprocal_sqrt, scale=EPS * EPS)
+
+        for a in range(2):
+            turn_weights(wv_raw[a], wv_grp[:, half_cols(a, PACK)], "m t u")
+        for h in range(2):
+            turn_weights(wk_raw[h], wk_grp[:, half_cols(h, PACK)], "t m u")
+
+        interleave(0, 0)
+        quantize(wv_codes, wv_scales, wv_grp, 0)
+        quantize_token(0, 0)
+        quantize(wv_codes, wv_scales, wv_grp, 1)
+        interleave(0, 1)
+        v_on_scalar(0, 0)
+        interleave(1, 0)
+        quantize_token(0, 1)
+        v_on_scalar(0, 1)
+        interleave(1, 1)
+        quantize_whole(wk_codes, wk_scales, wk_grp)
+        quantize_whole(tok_codes[1], tok_scales[1], tok_grp[1])
+        v_on_scalar(0, 2)
+        v_on_scalar(0, 3)
+        interleave(2, 0)
+        interleave(2, 1)
+        v_on_vector(1, 0)
+        squares(0, 0)
+        v_on_vector(1, 1)
+        squares(0, 1)
+        quantize_whole(tok_codes[2], tok_scales[2], tok_grp[2])
+        squares(0, 2)
+        v_on_vector(1, 2)
+        squares(0, 3)
+        spread_sumsq(0)
+        v_on_vector(1, 3)
+        squares(1, 0)
+        v_on_vector(2, 0)
+        squares(1, 1)
+        v_on_vector(2, 1)
+        invert_norm(0)
+        interleave(3, 0)
+        interleave(3, 1)
+        v_on_scalar(2, 2)
+        v_on_scalar(2, 3)
+        squares(1, 2)
+        squares(1, 3)
+        spread_sumsq(1)
+        k_tile(0, 0)
+        quantize_whole(tok_codes[3], tok_scales[3], tok_grp[3])
+        squares(2, 0)
+        k_tile(0, 1)
+        squares(2, 1)
+        k_tile(0, 2)
+        invert_norm(1)
+        k_tile(0, 3)
+        k_tile(1, 0)
+        squares(2, 2)
+        k_tile(1, 1)
+        squares(2, 3)
+        spread_sumsq(2)
+        k_tile(1, 2)
+        v_on_scalar(3, 0)
+        k_tile(1, 3)
+        squares(3, 0)
+        v_on_vector(3, 1)
+        v_on_vector(3, 2)
+        invert_norm(2)
+        k_tile(2, 0)
+        squares(3, 1)
+        k_tile(2, 1)
+        squares(3, 2)
+        k_tile(2, 2)
+        squares(3, 3)
+        spread_sumsq(3)
+        k_tile(2, 3)
+        v_on_vector(3, 3)
+        invert_norm(3)
+        k_tile(3, 0)
+        k_tile(3, 1)
+        k_tile(3, 2)
+        k_tile(3, 3)

@@ -40,6 +40,7 @@ def tile_trgramkqv_pa_kernel(tc, token, Wk, Wv, out_0, out_1):
         tiny = kept("tiny", [P, 1], F32)
         one = kept("one", [P, 1], F32)
         cap = kept("cap", [P, 1], F32)
+        idle = kept("idle", [P, 512], BF16)
         tok_raw = [kept("tok_raw%d" % b, [P, PACK, N], BF16) for b in range(B)]
         wv_grp = kept("wv_grp", [P, C * PACK], BF16)
         wk_grp = kept("wk_grp", [P, C * PACK], BF16)
@@ -194,15 +195,25 @@ def tile_trgramkqv_pa_kernel(tc, token, Wk, Wv, out_0, out_1):
             nc.sync.dma_start(out=wk_raw[h][:], in_=wk_rows[:, 2 * h : 2 * h + 2, :])
         for b in range(1, B):
             load_token(b)
+        nc.gpsimd.memset(idle[:].bitcast(U32), 0)
         nc.gpsimd.memset(one[:], 1.0)
         nc.gpsimd.memset(tiny[:], TINY)
         make_identity(nc, ident[:])
         nc.scalar.activation(out=cap[:], in_=one[:], func=ACT.Abs_reciprocal_sqrt, scale=EPS * EPS)
 
-        for a in range(2):
-            turn_weights(wv_raw[a], wv_grp[:, half_cols(a, PACK)], "m t u")
-        for h in range(2):
-            turn_weights(wk_raw[h], wk_grp[:, half_cols(h, PACK)], "t m u")
+        warm_bank = psum.tile([P, 512], F32, name="norm_bank", tag="norm_bank", bufs=1)
+
+        def warm_up(count):
+            for step in range(count):
+                nc.tensor.matmul(warm_bank[:], lhsT=idle[:, :P], rhs=idle[:], start=step == 0, stop=step == count - 1)
+
+        with tc.manual_schedule(engines={ENG.PE}):
+            warm_up(4)
+            for a in range(2):
+                turn_weights(wv_raw[a], wv_grp[:, half_cols(a, PACK)], "m t u")
+            warm_up(2)
+            for h in range(2):
+                turn_weights(wk_raw[h], wk_grp[:, half_cols(h, PACK)], "t m u")
 
         interleave(0, 0)
         quantize(wv_codes, wv_scales, wv_grp, 0)

@@ -39,8 +39,7 @@ def tile_trgramkqv_pa_kernel(tc, token, Wk, Wv, out_0, out_1):
         wk_raw = [kept("wk_raw%d" % h, [P, 2, K], BF16) for h in range(2)]
         tiny = kept("tiny", [P, 1], F32)
         one = kept("one", [P, 1], F32)
-        cap = kept("cap", [P, 1], F32)
-        idle = kept("idle", [P, 512], BF16)
+        root_tiny = kept("root_tiny", [P, 1], F32)
         tok_raw = [kept("tok_raw%d" % b, [P, PACK, N], BF16) for b in range(B)]
         wv_grp = kept("wv_grp", [P, C * PACK], BF16)
         wk_grp = kept("wk_grp", [P, C * PACK], BF16)
@@ -176,7 +175,7 @@ def tile_trgramkqv_pa_kernel(tc, token, Wk, Wv, out_0, out_1):
             nc.vector.scalar_tensor_tensor(
                 out=k_sb[b][:, t, :].rearrange("p (m i) -> p m i", i=2),
                 in0=inv_norm[b][:].rearrange("p (m i) -> p m i", i=2),
-                scalar=cap[:],
+                scalar=1.0 / EPS,
                 in1=bank[:].rearrange("p (i m) -> p m i", i=2),
                 op0=ALU.min,
                 op1=ALU.mult,
@@ -195,25 +194,15 @@ def tile_trgramkqv_pa_kernel(tc, token, Wk, Wv, out_0, out_1):
             nc.sync.dma_start(out=wk_raw[h][:], in_=wk_rows[:, 2 * h : 2 * h + 2, :])
         for b in range(1, B):
             load_token(b)
-        nc.gpsimd.memset(idle[:].bitcast(U32), 0)
         nc.gpsimd.memset(one[:], 1.0)
-        nc.gpsimd.memset(tiny[:], TINY)
         make_identity(nc, ident[:])
-        nc.scalar.activation(out=cap[:], in_=one[:], func=ACT.Abs_reciprocal_sqrt, scale=EPS * EPS)
+        nc.scalar.activation(out=root_tiny[:], in_=one[:], func=ACT.Abs_reciprocal_sqrt, scale=1.0 / TINY)
+        nc.scalar.activation(out=tiny[:], in_=root_tiny[:], func=ACT.Square)
 
-        warm_bank = psum.tile([P, 512], F32, name="norm_bank", tag="norm_bank", bufs=1)
-
-        def warm_up(count):
-            for step in range(count):
-                nc.tensor.matmul(warm_bank[:], lhsT=idle[:, :P], rhs=idle[:], start=step == 0, stop=step == count - 1)
-
-        with tc.manual_schedule(engines={ENG.PE}):
-            warm_up(4)
-            for a in range(2):
-                turn_weights(wv_raw[a], wv_grp[:, half_cols(a, PACK)], "m t u")
-            warm_up(2)
-            for h in range(2):
-                turn_weights(wk_raw[h], wk_grp[:, half_cols(h, PACK)], "t m u")
+        for a in range(2):
+            turn_weights(wv_raw[a], wv_grp[:, half_cols(a, PACK)], "m t u")
+        for h in range(2):
+            turn_weights(wk_raw[h], wk_grp[:, half_cols(h, PACK)], "t m u")
 
         interleave(0, 0)
         quantize(wv_codes, wv_scales, wv_grp, 0)
@@ -280,8 +269,8 @@ def tile_trgramkqv_pa_kernel(tc, token, Wk, Wv, out_0, out_1):
         k_tile(2, 2)
         squares(3, 3)
         spread_sumsq(3)
+        v_on_scalar(3, 3)
         k_tile(2, 3)
-        v_on_vector(3, 3)
         invert_norm(3)
         k_tile(3, 0)
         k_tile(3, 1)

@@ -5,6 +5,7 @@ from concourse.masks import make_identity
 
 B, C, K, N = 4, 512, 512, 512
 EPS = 1e-6
+TINY = 2.0**-80
 FLOPS = 2 * 2 * B * C * K * N
 
 F32 = mybir.dt.float32
@@ -15,12 +16,14 @@ E5M2X4 = mybir.dt.float8_e5m2_x4
 ACT = mybir.ActivationFunctionType
 ALU = mybir.AluOpType
 ENG = mybir.EngineType
-TINY = 2.0**-80
 
 P = 128
 PACK = 4
 TILES = 4
 HALF = 256
+BANK = 512
+SCALAR_BANKS, VECTOR_BANKS, NORM_BANKS = 4, 3, 1
+NORM_LAG = 2
 
 
 def tile_trgramkqv_pa_kernel(tc, token, Wk, Wv, out_0, out_1):
@@ -35,143 +38,137 @@ def tile_trgramkqv_pa_kernel(tc, token, Wk, Wv, out_0, out_1):
             return keep.tile(shape, dtype, name=name, align_bytes=64)
 
         ident = kept("ident", [P, P], F32)
-        wv_raw = [kept("wv_raw%d" % a, [P, 2, K], BF16) for a in range(2)]
-        wk_raw = [kept("wk_raw%d" % h, [P, 2, K], BF16) for h in range(2)]
-        tiny = kept("tiny", [P, 1], F32)
         one = kept("one", [P, 1], F32)
         root_tiny = kept("root_tiny", [P, 1], F32)
+        tiny = kept("tiny", [P, 1], F32)
+        wv_raw = [kept("wv_raw%d" % a, [P, 2, K], BF16) for a in range(2)]
+        wk_raw = [kept("wk_raw%d" % a, [P, 2, K], BF16) for a in range(2)]
         tok_raw = [kept("tok_raw%d" % b, [P, PACK, N], BF16) for b in range(B)]
-        wv_grp = kept("wv_grp", [P, C * PACK], BF16)
-        wk_grp = kept("wk_grp", [P, C * PACK], BF16)
-        tok_grp = [kept("tok_grp%d" % b, [P, N * PACK], BF16) for b in range(B)]
-        wv_codes = kept("wv_codes", [P, C], U32)
-        wv_scales = kept("wv_scales", [P, C], U8)
-        wk_codes = kept("wk_codes", [P, C], U32)
-        wk_scales = kept("wk_scales", [P, C], U8)
-        tok_codes = [kept("tok_codes%d" % b, [P, N], U32) for b in range(B)]
-        tok_scales = [kept("tok_scales%d" % b, [P, N], U8) for b in range(B)]
+        wv_grouped = kept("wv_grouped", [P, C * PACK], BF16)
+        wk_grouped = kept("wk_grouped", [P, C * PACK], BF16)
+        tok_grouped = [kept("tok_grouped%d" % b, [P, N * PACK], BF16) for b in range(B)]
+        wv_mx = (kept("wv_codes", [P, C], U32), kept("wv_scales", [P, C], U8))
+        wk_mx = (kept("wk_codes", [P, C], U32), kept("wk_scales", [P, C], U8))
+        tok_mx = [(kept("tok_codes%d" % b, [P, N], U32), kept("tok_scales%d" % b, [P, N], U8)) for b in range(B)]
         v_sb = [kept("v_sb%d" % b, [P, TILES, C], F32) for b in range(B)]
         k_sb = [kept("k_sb%d" % b, [P, TILES, N], F32) for b in range(B)]
         sumsq = [kept("sumsq%d" % b, [P, TILES], F32) for b in range(B)]
         inv_norm = [kept("inv_norm%d" % b, [P, N], F32) for b in range(B)]
+        spread_bank = {}
 
         def scalar_bank():
-            return psum.tile([P, 512], F32, name="scalar_bank", tag="scalar_bank", bufs=4)
+            return psum.tile([P, BANK], F32, name="scalar_bank", bufs=SCALAR_BANKS)
 
         def vector_bank():
-            return psum.tile([P, 512], F32, name="vector_bank", tag="vector_bank", bufs=3)
+            return psum.tile([P, BANK], F32, name="vector_bank", bufs=VECTOR_BANKS)
+
+        def norm_bank():
+            return psum.tile([P, BANK], F32, name="norm_bank", bufs=NORM_BANKS)
 
         def load_token(b):
-            nc.sync.dma_start(out=tok_raw[b][:], in_=token[b].rearrange("(p j) h w -> p j (h w)", j=PACK))
+            nc.sync.dma_start(out=tok_raw[b][:], in_=token[b].rearrange("(p t) h w -> p t (h w)", t=PACK))
 
-        def turn_weights(raw_pair, grp_half, order):
+        def turn_weights(raw, grouped, a, column_order):
             bank = scalar_bank()
-            turned = bank[:].rearrange("p (t u m) -> p t u m", t=2, u=2)
-            for t in range(2):
-                words = raw_pair[:, t, :].bitcast(F32)
+            turned = bank[:].rearrange("p (s u m) -> p s u m", s=2, u=2)
+            for s in range(2):
+                words = raw[:, s, :].bitcast(F32)
                 for u in range(2):
-                    nc.tensor.transpose(turned[:, t, u, :], words[:, u : 2 * P : 2], ident[:])
+                    nc.tensor.transpose(turned[:, s, u, :], words[:, u : 2 * P : 2], ident[:])
+            half_words = grouped[:, a * HALF * PACK : (a + 1) * HALF * PACK].bitcast(F32)
             nc.scalar.copy(
-                out=grp_half.bitcast(F32).rearrange("p (%s) -> p %s" % (order, order), t=2, u=2),
-                in_=turned.rearrange("p t u m -> p %s" % order),
+                out=half_words.rearrange("p (%s u) -> p %s u" % (column_order, column_order), s=2, u=2),
+                in_=turned.rearrange("p s u m -> p %s u" % column_order),
             )
 
-        def half_cols(a, scale=1):
-            return slice(a * HALF * scale, (a + 1) * HALF * scale)
-
-        def quantize(codes, scales, grp, a):
+        def quantize(mx, grouped, first, width):
+            codes, scales = mx
             nc.vector.quantize_mx(
-                out=codes[:, half_cols(a)].bitcast(E5M2X4),
-                scales=scales[:, half_cols(a)],
-                in_=grp[:, half_cols(a, PACK)],
+                out=codes[:, first : first + width].bitcast(E5M2X4),
+                scales=scales[:, first : first + width],
+                in_=grouped[:, first * PACK : (first + width) * PACK],
             )
 
-        def quantize_whole(codes, scales, grp):
-            nc.vector.quantize_mx(out=codes[:].bitcast(E5M2X4), scales=scales[:], in_=grp[:])
-
-        def interleave(b, a):
-            grouped = tok_grp[b][:].rearrange("p (i a c m t) -> p a c t m i", i=2, a=2, m=2, t=PACK)
+        def group_token(b, a):
+            grouped = tok_grouped[b][:].rearrange("p (i a c e t) -> p a c t e i", i=2, a=2, e=2, t=PACK)
             nc.vector.tensor_copy(
                 out=grouped[:, a],
-                in_=tok_raw[b][:, :, half_cols(a)].rearrange("p t (c m i) -> p c t m i", m=2, i=2),
+                in_=tok_raw[b][:, :, a * HALF : (a + 1) * HALF].rearrange("p t (c e i) -> p c t e i", e=2, i=2),
             )
 
-        def pixel_block(j):
-            return 2 * (j % 2) + j // 2
+        def token_column(j):
+            return HALF * (j % 2) + P * (j // 2)
 
-        def quantize_token(b, a):
-            for i in range(2):
-                first = pixel_block(2 * a + i) * P
-                nc.vector.quantize_mx(
-                    out=tok_codes[b][:, first : first + P].bitcast(E5M2X4),
-                    scales=tok_scales[b][:, first : first + P],
-                    in_=tok_grp[b][:, first * PACK : (first + P) * PACK],
-                )
+        def quantize_token(b):
+            quantize(tok_mx[b], tok_grouped[b], 0, N)
 
-        def product(bank, lhs_codes, lhs_scales, j, rhs_codes, rhs_scales):
-            cols = slice(j * P, (j + 1) * P)
+        def quantize_token_half(b, a):
+            for j in (2 * a, 2 * a + 1):
+                quantize(tok_mx[b], tok_grouped[b], token_column(j), P)
+
+        def product(bank, stationary, first, moving):
             nc.tensor.matmul_mx(
                 out=bank[:],
-                lhsT=lhs_codes[:, cols].bitcast(E5M2X4),
-                lhsT_scale=lhs_scales[:, cols],
-                rhs=rhs_codes[:].bitcast(E5M2X4),
-                rhs_scale=rhs_scales[:],
+                lhsT=stationary[0][:, first : first + P].bitcast(E5M2X4),
+                lhsT_scale=stationary[1][:, first : first + P],
+                rhs=moving[0][:].bitcast(E5M2X4),
+                rhs_scale=moving[1][:],
                 start=True,
                 stop=True,
             )
 
-        def store_v(b, a):
-            nc.sync.dma_start(
-                out=out_1[b].rearrange("(a m i) c -> m a i c", a=2, i=2)[:, a, :, :],
-                in_=v_sb[b][:, 2 * a : 2 * a + 2, :],
-            )
+        def store_v_half(b, a):
+            rows = out_1[b].rearrange("(a m i) c -> m a i c", a=2, i=2)
+            nc.sync.dma_start(out=rows[:, a, :, :], in_=v_sb[b][:, 2 * a : 2 * a + 2, :])
 
         def store_k(b, t, count):
-            nc.sync.dma_start(
-                out=out_0[b].rearrange("(m t) n -> m t n", t=TILES)[:, t : t + count, :],
-                in_=k_sb[b][:, t : t + count, :],
-            )
+            rows = out_0[b].rearrange("(m t) n -> m t n", t=TILES)
+            nc.sync.dma_start(out=rows[:, t : t + count, :], in_=k_sb[b][:, t : t + count, :])
 
-        def v_on_scalar(b, j):
-            bank = scalar_bank()
-            product(bank, tok_codes[b], tok_scales[b], pixel_block(j), wv_codes, wv_scales)
-            nc.scalar.copy(out=v_sb[b][:, j, :], in_=bank[:])
+        def v_tile(b, j, bank, copy):
+            product(bank, tok_mx[b], token_column(j), wv_mx)
+            copy(out=v_sb[b][:, j, :], in_=bank[:])
             if j % 2 == 1:
-                store_v(b, j // 2)
+                store_v_half(b, j // 2)
 
-        def v_on_vector(b, j):
-            bank = vector_bank()
-            product(bank, tok_codes[b], tok_scales[b], pixel_block(j), wv_codes, wv_scales)
-            nc.vector.tensor_copy(out=v_sb[b][:, j, :], in_=bank[:])
-            if j % 2 == 1:
-                store_v(b, j // 2)
+        def v_half_on_scalar(b, a):
+            for j in (2 * a, 2 * a + 1):
+                v_tile(b, j, scalar_bank(), nc.scalar.copy)
 
-        def squares(b, j):
+        def v_tile_on_vector(b, j):
+            v_tile(b, j, vector_bank(), nc.vector.tensor_copy)
+
+        def squares_tile(b, j):
             bank = scalar_bank()
-            product(bank, tok_codes[b], tok_scales[b], pixel_block(j), wk_codes, wk_scales)
+            product(bank, tok_mx[b], token_column(j), wk_mx)
             squared = scratch.tile([P, C], F32, name="squared")
             nc.scalar.activation(out=squared[:], in_=bank[:], func=ACT.Square, accum_out=sumsq[b][:, j : j + 1])
+            if b < B - 1 and j == TILES - 1:
+                whole = norm_bank()
+                spread_sums(b, 0, whole)
+                spread_sums(b, 1, whole)
+            elif b == B - 1 and j % 2 == 1:
+                spread_sums(b, j // 2, norm_bank() if j == 1 else scalar_bank())
 
-        norm_banks = {}
+        def spread_sums(b, a, bank):
+            for j in (2 * a, 2 * a + 1):
+                first = token_column(j)
+                repeated = sumsq[b][:, j : j + 1].to_broadcast([P, P])
+                nc.tensor.transpose(bank[:, first : first + P], repeated, ident[:])
+            spread_bank[b, a] = bank
 
-        def spread_sumsq(b):
-            bank = psum.tile([P, 512], F32, name="norm_bank", tag="norm_bank", bufs=1)
-            for j in range(TILES):
-                first = pixel_block(j) * P
-                nc.tensor.transpose(bank[:, first : first + P], sumsq[b][:, j : j + 1].to_broadcast([P, P]), ident[:])
-            norm_banks[b] = bank
-
-        def invert_norm(b):
+        def invert_norm(b, first_half, halves):
+            rows = slice(first_half * P, (first_half + halves) * P)
             nc.scalar.activation(
-                out=inv_norm[b][:].rearrange("p (m i) -> p m i", i=2),
-                in_=norm_banks[b][:].rearrange("p (i m) -> p m i", i=2),
+                out=inv_norm[b][:].rearrange("p (m i) -> p m i", i=2)[:, rows, :],
+                in_=spread_bank[b, first_half][:].rearrange("p (i m) -> p m i", i=2)[:, rows, :],
                 func=ACT.Abs_reciprocal_sqrt,
                 bias=tiny[:],
             )
 
         def k_tile(b, t):
             bank = vector_bank()
-            product(bank, wk_codes, wk_scales, t, tok_codes[b], tok_scales[b])
+            product(bank, wk_mx, t * P, tok_mx[b])
             nc.vector.scalar_tensor_tensor(
                 out=k_sb[b][:, t, :].rearrange("p (m i) -> p m i", i=2),
                 in0=inv_norm[b][:].rearrange("p (m i) -> p m i", i=2),
@@ -185,94 +182,61 @@ def tile_trgramkqv_pa_kernel(tc, token, Wk, Wv, out_0, out_1):
             elif t % 2 == 1:
                 store_k(b, t - 1, 2)
 
-        wv_rows = Wv.rearrange("(a m t) k -> m a t k", a=2, t=2)
+        wv_rows = Wv.rearrange("(a m s) k -> m a s k", a=2, s=2)
+        wk_rows = Wk.rearrange("(m a s) k -> m a s k", a=2, s=2)
         for a in range(2):
             nc.sync.dma_start(out=wv_raw[a][:], in_=wv_rows[:, a, :, :])
         load_token(0)
-        wk_rows = Wk.rearrange("(m t) k -> m t k", t=PACK)
-        for h in range(2):
-            nc.sync.dma_start(out=wk_raw[h][:], in_=wk_rows[:, 2 * h : 2 * h + 2, :])
+        for a in range(2):
+            nc.sync.dma_start(out=wk_raw[a][:], in_=wk_rows[:, a, :, :])
         for b in range(1, B):
             load_token(b)
+
         nc.gpsimd.memset(one[:], 1.0)
         make_identity(nc, ident[:])
         nc.scalar.activation(out=root_tiny[:], in_=one[:], func=ACT.Abs_reciprocal_sqrt, scale=1.0 / TINY)
         nc.scalar.activation(out=tiny[:], in_=root_tiny[:], func=ACT.Square)
 
         for a in range(2):
-            turn_weights(wv_raw[a], wv_grp[:, half_cols(a, PACK)], "m t u")
-        for h in range(2):
-            turn_weights(wk_raw[h], wk_grp[:, half_cols(h, PACK)], "t m u")
+            turn_weights(wv_raw[a], wv_grouped, a, "m s")
+        for a in range(2):
+            turn_weights(wk_raw[a], wk_grouped, a, "s m")
 
-        interleave(0, 0)
-        quantize(wv_codes, wv_scales, wv_grp, 0)
-        quantize_token(0, 0)
-        quantize(wv_codes, wv_scales, wv_grp, 1)
-        interleave(0, 1)
-        v_on_scalar(0, 0)
-        interleave(1, 0)
-        quantize_token(0, 1)
-        v_on_scalar(0, 1)
-        interleave(1, 1)
-        quantize_whole(wk_codes, wk_scales, wk_grp)
-        quantize_whole(tok_codes[1], tok_scales[1], tok_grp[1])
-        v_on_scalar(0, 2)
-        v_on_scalar(0, 3)
-        interleave(2, 0)
-        interleave(2, 1)
-        v_on_vector(1, 0)
-        squares(0, 0)
-        v_on_vector(1, 1)
-        squares(0, 1)
-        quantize_whole(tok_codes[2], tok_scales[2], tok_grp[2])
-        squares(0, 2)
-        v_on_vector(1, 2)
-        squares(0, 3)
-        spread_sumsq(0)
-        v_on_vector(1, 3)
-        squares(1, 0)
-        v_on_vector(2, 0)
-        squares(1, 1)
-        v_on_vector(2, 1)
-        invert_norm(0)
-        interleave(3, 0)
-        interleave(3, 1)
-        v_on_scalar(2, 2)
-        v_on_scalar(2, 3)
-        squares(1, 2)
-        squares(1, 3)
-        spread_sumsq(1)
-        k_tile(0, 0)
-        quantize_whole(tok_codes[3], tok_scales[3], tok_grp[3])
-        squares(2, 0)
-        k_tile(0, 1)
-        squares(2, 1)
-        k_tile(0, 2)
-        invert_norm(1)
-        k_tile(0, 3)
-        k_tile(1, 0)
-        squares(2, 2)
-        k_tile(1, 1)
-        squares(2, 3)
-        spread_sumsq(2)
-        k_tile(1, 2)
-        v_on_scalar(3, 0)
-        k_tile(1, 3)
-        squares(3, 0)
-        v_on_vector(3, 1)
-        v_on_vector(3, 2)
-        invert_norm(2)
-        k_tile(2, 0)
-        squares(3, 1)
-        k_tile(2, 1)
-        squares(3, 2)
-        k_tile(2, 2)
-        squares(3, 3)
-        spread_sumsq(3)
-        v_on_scalar(3, 3)
-        k_tile(2, 3)
-        invert_norm(3)
-        k_tile(3, 0)
-        k_tile(3, 1)
-        k_tile(3, 2)
-        k_tile(3, 3)
+        group_token(0, 0)
+        quantize(wv_mx, wv_grouped, 0, HALF)
+        quantize_token_half(0, 0)
+        quantize(wv_mx, wv_grouped, HALF, HALF)
+        v_half_on_scalar(0, 0)
+        group_token(0, 1)
+        quantize_token_half(0, 1)
+        v_half_on_scalar(0, 1)
+        for a in range(2):
+            group_token(1, a)
+        for a in range(2):
+            quantize_token_half(1, a)
+            v_half_on_scalar(1, a)
+            group_token(2, a)
+        quantize(wk_mx, wk_grouped, 0, C)
+        quantize_token(2)
+        for a in range(2):
+            group_token(3, a)
+
+        scalar_steps = []
+        for b in range(B):
+            for j in range(TILES):
+                if b > 0 and j == NORM_LAG:
+                    scalar_steps.append((invert_norm, (b - 1, 0, 2)))
+                scalar_steps.append((squares_tile, (b, j)))
+        scalar_steps.extend((invert_norm, (B - 1, a, 1)) for a in range(2))
+
+        vector_steps = [(v_tile_on_vector, (2, j)) for j in range(2)]
+        vector_steps.append((quantize_token, (3,)))
+        vector_steps.extend((v_tile_on_vector, (2, j)) for j in range(2, TILES))
+        vector_steps.extend((v_tile_on_vector, (3, j)) for j in range(TILES))
+        vector_steps.extend((k_tile, (b, t)) for b in range(B) for t in range(TILES))
+
+        for step in range(len(vector_steps)):
+            for steps in (scalar_steps, vector_steps):
+                if step < len(steps):
+                    call, args = steps[step]
+                    call(*args)

from contextlib import ExitStack

import concourse.mybir as mybir
from concourse.masks import make_identity

B, C, K, N = 4, 512, 512, 512
EPS = 1e-6
TINY = 2.0**-80
FLOPS = 2 * 2 * B * C * K * N

F32 = mybir.dt.float32
BF16 = mybir.dt.bfloat16
U32 = mybir.dt.uint32
U8 = mybir.dt.uint8
E5M2X4 = mybir.dt.float8_e5m2_x4
ACT = mybir.ActivationFunctionType
ALU = mybir.AluOpType
ENG = mybir.EngineType

P = 128
PACK = 4
TILES = 4
HALF = 256
BANK = 512
SCALAR_BANKS, VECTOR_BANKS, NORM_BANKS = 4, 3, 1
NORM_LAG = 2


def tile_trgramkqv_pa_kernel(tc, token, Wk, Wv, out_0, out_1):
    nc = tc.nc
    with ExitStack() as ctx:
        keep = ctx.enter_context(tc.tile_pool(name="keep", bufs=1))
        scratch = ctx.enter_context(tc.tile_pool(name="scratch", bufs=2))
        psum = ctx.enter_context(tc.psum_pool(name="psum", bufs=1))
        ctx.enter_context(tc.manual_schedule(engines={ENG.Activation, ENG.DVE, ENG.SP, ENG.Pool}))

        def kept(name, shape, dtype):
            return keep.tile(shape, dtype, name=name, align_bytes=64)

        ident = kept("ident", [P, P], F32)
        one = kept("one", [P, 1], F32)
        root_tiny = kept("root_tiny", [P, 1], F32)
        tiny = kept("tiny", [P, 1], F32)
        wv_raw = [kept("wv_raw%d" % a, [P, 2, K], BF16) for a in range(2)]
        wk_raw = [kept("wk_raw%d" % a, [P, 2, K], BF16) for a in range(2)]
        tok_raw = [kept("tok_raw%d" % b, [P, PACK, N], BF16) for b in range(B)]
        wv_grouped = kept("wv_grouped", [P, C * PACK], BF16)
        wk_grouped = kept("wk_grouped", [P, C * PACK], BF16)
        tok_grouped = [kept("tok_grouped%d" % b, [P, N * PACK], BF16) for b in range(B)]
        wv_mx = (kept("wv_codes", [P, C], U32), kept("wv_scales", [P, C], U8))
        wk_mx = (kept("wk_codes", [P, C], U32), kept("wk_scales", [P, C], U8))
        tok_mx = [(kept("tok_codes%d" % b, [P, N], U32), kept("tok_scales%d" % b, [P, N], U8)) for b in range(B)]
        v_sb = [kept("v_sb%d" % b, [P, TILES, C], F32) for b in range(B)]
        k_sb = [kept("k_sb%d" % b, [P, TILES, N], F32) for b in range(B)]
        sumsq = [kept("sumsq%d" % b, [P, TILES], F32) for b in range(B)]
        inv_norm = [kept("inv_norm%d" % b, [P, N], F32) for b in range(B)]
        spread_bank = {}

        def scalar_bank():
            return psum.tile([P, BANK], F32, name="scalar_bank", bufs=SCALAR_BANKS)

        def vector_bank():
            return psum.tile([P, BANK], F32, name="vector_bank", bufs=VECTOR_BANKS)

        def norm_bank():
            return psum.tile([P, BANK], F32, name="norm_bank", bufs=NORM_BANKS)

        def load_token(b):
            nc.sync.dma_start(out=tok_raw[b][:], in_=token[b].rearrange("(p t) h w -> p t (h w)", t=PACK))

        def turn_weights(raw, grouped, a, column_order):
            bank = scalar_bank()
            turned = bank[:].rearrange("p (s u m) -> p s u m", s=2, u=2)
            for s in range(2):
                words = raw[:, s, :].bitcast(F32)
                for u in range(2):
                    nc.tensor.transpose(turned[:, s, u, :], words[:, u : 2 * P : 2], ident[:])
            half_words = grouped[:, a * HALF * PACK : (a + 1) * HALF * PACK].bitcast(F32)
            nc.scalar.copy(
                out=half_words.rearrange("p (%s u) -> p %s u" % (column_order, column_order), s=2, u=2),
                in_=turned.rearrange("p s u m -> p %s u" % column_order),
            )

        def quantize(mx, grouped, first, width):
            codes, scales = mx
            nc.vector.quantize_mx(
                out=codes[:, first : first + width].bitcast(E5M2X4),
                scales=scales[:, first : first + width],
                in_=grouped[:, first * PACK : (first + width) * PACK],
            )

        def group_token(b, a):
            grouped = tok_grouped[b][:].rearrange("p (i a c e t) -> p a c t e i", i=2, a=2, e=2, t=PACK)
            nc.vector.tensor_copy(
                out=grouped[:, a],
                in_=tok_raw[b][:, :, a * HALF : (a + 1) * HALF].rearrange("p t (c e i) -> p c t e i", e=2, i=2),
            )

        def token_column(j):
            return HALF * (j % 2) + P * (j // 2)

        def quantize_token(b):
            quantize(tok_mx[b], tok_grouped[b], 0, N)

        def quantize_token_half(b, a):
            for j in (2 * a, 2 * a + 1):
                quantize(tok_mx[b], tok_grouped[b], token_column(j), P)

        def product(bank, stationary, first, moving):
            nc.tensor.matmul_mx(
                out=bank[:],
                lhsT=stationary[0][:, first : first + P].bitcast(E5M2X4),
                lhsT_scale=stationary[1][:, first : first + P],
                rhs=moving[0][:].bitcast(E5M2X4),
                rhs_scale=moving[1][:],
                start=True,
                stop=True,
            )

        def store_v_half(b, a):
            rows = out_1[b].rearrange("(a m i) c -> m a i c", a=2, i=2)
            nc.sync.dma_start(out=rows[:, a, :, :], in_=v_sb[b][:, 2 * a : 2 * a + 2, :])

        def store_k(b, t, count):
            rows = out_0[b].rearrange("(m t) n -> m t n", t=TILES)
            nc.sync.dma_start(out=rows[:, t : t + count, :], in_=k_sb[b][:, t : t + count, :])

        def v_tile(b, j, bank, copy):
            product(bank, tok_mx[b], token_column(j), wv_mx)
            copy(out=v_sb[b][:, j, :], in_=bank[:])
            if j % 2 == 1:
                store_v_half(b, j // 2)

        def v_half_on_scalar(b, a):
            for j in (2 * a, 2 * a + 1):
                v_tile(b, j, scalar_bank(), nc.scalar.copy)

        def v_tile_on_vector(b, j):
            v_tile(b, j, vector_bank(), nc.vector.tensor_copy)

        def squares_tile(b, j):
            bank = scalar_bank()
            product(bank, tok_mx[b], token_column(j), wk_mx)
            squared = scratch.tile([P, C], F32, name="squared")
            nc.scalar.activation(out=squared[:], in_=bank[:], func=ACT.Square, accum_out=sumsq[b][:, j : j + 1])
            if b < B - 1 and j == TILES - 1:
                whole = norm_bank()
                spread_sums(b, 0, whole)
                spread_sums(b, 1, whole)
            elif b == B - 1 and j % 2 == 1:
                spread_sums(b, j // 2, norm_bank() if j == 1 else scalar_bank())

        def spread_sums(b, a, bank):
            for j in (2 * a, 2 * a + 1):
                first = token_column(j)
                repeated = sumsq[b][:, j : j + 1].to_broadcast([P, P])
                nc.tensor.transpose(bank[:, first : first + P], repeated, ident[:])
            spread_bank[b, a] = bank

        def invert_norm(b, first_half, halves):
            rows = slice(first_half * P, (first_half + halves) * P)
            nc.scalar.activation(
                out=inv_norm[b][:].rearrange("p (m i) -> p m i", i=2)[:, rows, :],
                in_=spread_bank[b, first_half][:].rearrange("p (i m) -> p m i", i=2)[:, rows, :],
                func=ACT.Abs_reciprocal_sqrt,
                bias=tiny[:],
            )

        def k_tile(b, t):
            bank = vector_bank()
            product(bank, wk_mx, t * P, tok_mx[b])
            nc.vector.scalar_tensor_tensor(
                out=k_sb[b][:, t, :].rearrange("p (m i) -> p m i", i=2),
                in0=inv_norm[b][:].rearrange("p (m i) -> p m i", i=2),
                scalar=1.0 / EPS,
                in1=bank[:].rearrange("p (i m) -> p m i", i=2),
                op0=ALU.min,
                op1=ALU.mult,
            )
            if b == B - 1 and t >= 2:
                store_k(b, t, 1)
            elif t % 2 == 1:
                store_k(b, t - 1, 2)

        wv_rows = Wv.rearrange("(a m s) k -> m a s k", a=2, s=2)
        wk_rows = Wk.rearrange("(m a s) k -> m a s k", a=2, s=2)
        for a in range(2):
            nc.sync.dma_start(out=wv_raw[a][:], in_=wv_rows[:, a, :, :])
        load_token(0)
        for a in range(2):
            nc.sync.dma_start(out=wk_raw[a][:], in_=wk_rows[:, a, :, :])
        for b in range(1, B):
            load_token(b)

        nc.gpsimd.memset(one[:], 1.0)
        make_identity(nc, ident[:])
        nc.scalar.activation(out=root_tiny[:], in_=one[:], func=ACT.Abs_reciprocal_sqrt, scale=1.0 / TINY)
        nc.scalar.activation(out=tiny[:], in_=root_tiny[:], func=ACT.Square)

        for a in range(2):
            turn_weights(wv_raw[a], wv_grouped, a, "m s")
        for a in range(2):
            turn_weights(wk_raw[a], wk_grouped, a, "s m")

        group_token(0, 0)
        quantize(wv_mx, wv_grouped, 0, HALF)
        quantize_token_half(0, 0)
        quantize(wv_mx, wv_grouped, HALF, HALF)
        v_half_on_scalar(0, 0)
        group_token(0, 1)
        quantize_token_half(0, 1)
        v_half_on_scalar(0, 1)
        for a in range(2):
            group_token(1, a)
        for a in range(2):
            quantize_token_half(1, a)
            v_half_on_scalar(1, a)
            group_token(2, a)
        quantize(wk_mx, wk_grouped, 0, C)
        quantize_token(2)
        for a in range(2):
            group_token(3, a)

        scalar_steps = []
        for b in range(B):
            for j in range(TILES):
                if b > 0 and j == NORM_LAG:
                    scalar_steps.append((invert_norm, (b - 1, 0, 2)))
                scalar_steps.append((squares_tile, (b, j)))
        scalar_steps.extend((invert_norm, (B - 1, a, 1)) for a in range(2))

        vector_steps = [(v_tile_on_vector, (2, j)) for j in range(2)]
        vector_steps.append((quantize_token, (3,)))
        vector_steps.extend((v_tile_on_vector, (2, j)) for j in range(2, TILES))
        vector_steps.extend((v_tile_on_vector, (3, j)) for j in range(TILES))
        vector_steps.extend((k_tile, (b, t)) for b in range(B) for t in range(TILES))

        for step in range(len(vector_steps)):
            for steps in (scalar_steps, vector_steps):
                if step < len(steps):
                    call, args = steps[step]
                    call(*args)
